import numpy as np
import ml_dtypes


def mxq(x, axis, fmt="e4m3"):
    dtype, down = {"e4m3": (ml_dtypes.float8_e4m3fn, 7), "e5m2": (ml_dtypes.float8_e5m2, 14)}[fmt]
    v = np.moveaxis(np.asarray(x, np.float32).astype(ml_dtypes.bfloat16).astype(np.float64), axis, -1)
    blocks = v.reshape(v.shape[:-1] + (-1, 32))
    amax = np.abs(blocks).max(-1, keepdims=True)
    byte = np.maximum(np.where(amax > 0, np.frexp(amax)[1] - 1 + 127, 0) - down, 1)
    scale = np.exp2(byte - 127.0)
    codes = (blocks / scale).astype(np.float32).astype(dtype).astype(np.float64)
    return np.moveaxis((codes * scale).reshape(v.shape), -1, axis)


WIDE = False


def mx_kscale(k):
    if not WIDE:
        return np.ones(k)
    levels = np.array([10, -10, 5, -5, 0])
    a = np.random.permutation(np.resize(levels, k // 512 * 4)).reshape(k // 512, 4)
    idx = np.arange(k)
    return np.exp2(a[idx // 512, idx % 128 // 32])


BF16 = ml_dtypes.bfloat16


def bf(x):
    return np.asarray(x, np.float32).astype(BF16)


def f64(x):
    return np.asarray(x).astype(np.float64)


B, T, D, C, M = 2, 1024, 1024, 128, 4
NB = T // M
NEG = -1e30


def setup_inputs():
    s = mx_kscale(D)
    w = 1.0 / np.sqrt(D)
    return {
        "H": bf(np.random.standard_normal((B, T, D)) * s),
        "W_a_KV": bf(np.random.standard_normal((D, C)) * w / s[:, None]),
        "W_b_KV": bf(np.random.standard_normal((D, C)) * w / s[:, None]),
        "W_a_Z": bf(np.random.standard_normal((D, C)) * w / s[:, None]),
        "W_b_Z": bf(np.random.standard_normal((D, C)) * w / s[:, None]),
        "B_a": bf(np.random.standard_normal((M, C))),
        "B_b": bf(np.random.standard_normal((M, C))),
    }


def reference(H, W_a_KV, W_b_KV, W_a_Z, W_b_Z, B_a, B_b):
    Hq = mxq(f64(H), 2, "e4m3")
    C_a = (Hq @ mxq(f64(W_a_KV), 0, "e4m3")).reshape(B, NB, M, C)
    C_b = (Hq @ mxq(f64(W_b_KV), 0, "e4m3")).reshape(B, NB, M, C)
    Z_a = (Hq @ mxq(f64(W_a_Z), 0, "e4m3")).reshape(B, NB, M, C) + f64(B_a)
    Z_b = (Hq @ mxq(f64(W_b_Z), 0, "e4m3")).reshape(B, NB, M, C) + f64(B_b)
    Z_b_prev = np.concatenate([np.full((B, 1, M, C), NEG), Z_b[:, :-1]], axis=1)
    C_b_prev = np.concatenate([np.zeros((B, 1, M, C)), C_b[:, :-1]], axis=1)
    logits = np.concatenate([Z_a, Z_b_prev], axis=2)
    vals = np.concatenate([C_a, C_b_prev], axis=2)
    e = np.exp(logits - logits.max(axis=2, keepdims=True))
    probs = e / e.sum(axis=2, keepdims=True)
    return (probs * vals).sum(axis=2)

@@ -1,0 +1,200 @@
+from contextlib import ExitStack
+
+import concourse.mybir as mybir
+from concourse.masks import make_identity
+
+F32 = mybir.dt.float32
+BF16 = mybir.dt.bfloat16
+U32 = mybir.dt.uint32
+U8 = mybir.dt.uint8
+FP8X4 = mybir.dt.float8_e4m3fn_x4
+ACT = mybir.ActivationFunctionType
+ALU = mybir.AluOpType
+
+P = 128
+BATCH = 2
+TOKENS = 1024
+D = 1024
+CH = 128
+M = 4
+K_PASS = 512
+PASSES = D // K_PASS
+GROUP = 128
+GROUPS = BATCH * TOKENS // (M * GROUP)
+GROUPS_PER_BATCH = GROUPS // BATCH
+BLOCKS = TOKENS // M
+NEG = -1e30
+
+FLOPS = 2 * BATCH * TOKENS * D * 4 * CH
+
+
+def tile_tokencompressor_pa_kernel(tc, H, W_a_KV, W_b_KV, W_a_Z, W_b_Z, B_a, B_b, out):
+    nc = tc.nc
+    weights = [W_a_Z, W_b_Z, W_a_KV, W_b_KV]
+    h_groups = H.flatten_outer_dims().rearrange("(g i j) d -> g i j d", i=GROUP, j=M)
+    out_rows = out.flatten_outer_dims().rearrange("(g i) c -> i g c", i=GROUP)
+
+    with ExitStack() as stack:
+        keep = stack.enter_context(tc.tile_pool(name="keep", bufs=1))
+        work = stack.enter_context(tc.tile_pool(name="work", bufs=2))
+        psum = stack.enter_context(tc.psum_pool(name="psum", bufs=1))
+
+        h_raw = [keep.tile([P, M, D], BF16, name="h_raw%d" % g) for g in range(GROUPS)]
+        w_raw = keep.tile([P, 4, PASSES, 4, CH], BF16)
+
+        def load_h(g):
+            for half in range(2):
+                js = slice(2 * half, 2 * half + 2)
+                nc.sync.dma_start(out=h_raw[g][:, js, :], in_=h_groups[g][:, js, :])
+
+        load_h(0)
+        for w in range(4):
+            nc.sync.dma_start(
+                out=w_raw[:, w].rearrange("p c (u e) n -> p c u e n", e=2),
+                in_=weights[w].rearrange("(c u p e) n -> p c u e n", c=PASSES, u=2, e=2),
+            )
+        for g in range(1, GROUPS):
+            load_h(g)
+
+        ident = keep.tile([P, P], F32)
+        make_identity(nc, ident[:])
+
+        bias_rows = keep.tile([P, P], BF16)
+        nc.vector.memset(bias_rows[:], 0.0)
+        nc.scalar.dma_start(out=bias_rows[0:M, :], in_=B_a)
+        nc.scalar.dma_start(out=bias_rows[M : 2 * M, :], in_=B_b)
+        bias_rows32 = keep.tile([P, P], F32)
+        nc.vector.tensor_copy(out=bias_rows32[:], in_=bias_rows[:])
+        bias_ps = psum.tile([P, P], F32, tag="tp")
+        nc.tensor.transpose(out=bias_ps[:], in_=bias_rows32[:], identity=ident[:])
+        bias = keep.tile([P, 2 * M], F32)
+        nc.vector.tensor_copy(out=bias[:], in_=bias_ps[:, 0 : 2 * M])
+
+        z_all = [keep.tile([P, 2 * M, BLOCKS + 1], F32, name="z_all%d" % n) for n in range(BATCH)]
+        cb_all = [keep.tile([P, M, BLOCKS + 1], F32, name="cb_all%d" % n) for n in range(BATCH)]
+        for n in range(BATCH):
+            nc.vector.memset(z_all[n][:, M : 2 * M, 0:1], NEG)
+            nc.vector.memset(cb_all[n][:, :, 0:1], 0.0)
+        sums = keep.tile([P, 2, GROUPS * GROUP], F32)
+
+        w_grouped = keep.tile([P, 4, PASSES, CH, 4], BF16, align_bytes=64)
+        w_codes = keep.tile([P, 4, PASSES, CH], U32, align_bytes=64)
+        w_scales = keep.tile([P, 4, PASSES, CH], U8, align_bytes=64)
+        for w in range(4):
+            nc.vector.tensor_copy(out=w_grouped[:, w], in_=w_raw[:, w].rearrange("p c t n -> p c n t"))
+        for w in range(4):
+            nc.vector.quantize_mx(
+                out=w_codes[:, w].rearrange("p c n -> p (c n)").bitcast(FP8X4),
+                scales=w_scales[:, w].rearrange("p c n -> p (c n)"),
+                in_=w_grouped[:, w].rearrange("p c n t -> p (c n t)"),
+            )
+
+        def quantise_h(g):
+            h_words = h_raw[g].bitcast(F32)
+            h_grouped = work.tile([P, PASSES, M * GROUP, 4], BF16, align_bytes=64)
+            h_grouped_words = h_grouped.bitcast(F32)
+            h_codes = work.tile([P, PASSES, M * GROUP], U32, align_bytes=64)
+            h_scales = work.tile([P, PASSES, M * GROUP], U8, align_bytes=64)
+            for c in range(PASSES):
+                for half in range(2):
+                    xt = psum.tile([P, 2, 2, GROUP], F32, tag="xt", bufs=3)
+                    for u in range(2):
+                        for jj in range(2):
+                            first = 256 * c + 128 * u
+                            nc.tensor.transpose(
+                                out=xt[:, u, jj, :],
+                                in_=h_words[:, 2 * half + jj, first : first + 128],
+                                identity=ident[:],
+                            )
+                    cols = slice(2 * GROUP * half, 2 * GROUP * (half + 1))
+                    nc.scalar.copy(
+                        out=h_grouped_words[:, c, cols, :],
+                        in_=xt.rearrange("p u jj i -> p (jj i) u"),
+                    )
+                nc.vector.quantize_mx(
+                    out=h_codes[:, c, :].bitcast(FP8X4),
+                    scales=h_scales[:, c, :],
+                    in_=h_grouped[:, c].rearrange("p col t -> p (col t)"),
+                )
+            return h_codes, h_scales
+
+        def project(w, h_codes, h_scales, tag):
+            acc = psum.tile([P, M, GROUP], F32, tag=tag)
+            for c in range(PASSES):
+                nc.tensor.matmul_mx(
+                    out=acc.rearrange("p j i -> p (j i)"),
+                    lhsT=w_codes[:, w, c, :].bitcast(FP8X4),
+                    lhsT_scale=w_scales[:, w, c, :],
+                    rhs=h_codes[:, c, :].bitcast(FP8X4),
+                    rhs_scale=h_scales[:, c, :],
+                    start=(c == 0),
+                    stop=(c == PASSES - 1),
+                )
+            return acc
+
+        quantised = quantise_h(0)
+        for g in range(GROUPS):
+            n = g // GROUPS_PER_BATCH
+            first = GROUP * (g % GROUPS_PER_BATCH)
+            h_codes, h_scales = quantised
+            za = project(0, h_codes, h_scales, "za")
+            zb = project(1, h_codes, h_scales, "zb")
+            ca = project(2, h_codes, h_scales, "ca")
+            cb = project(3, h_codes, h_scales, "cb")
+            if g + 1 < GROUPS:
+                quantised = quantise_h(g + 1)
+
+            for j in range(M):
+                nc.scalar.activation(
+                    out=z_all[n][:, j, first : first + GROUP], in_=za[:, j, :],
+                    func=ACT.Identity, bias=bias[:, j : j + 1], scale=1.0,
+                )
+            for j in range(M):
+                nc.scalar.activation(
+                    out=z_all[n][:, M + j, first + 1 : first + 1 + GROUP], in_=zb[:, j, :],
+                    func=ACT.Identity, bias=bias[:, M + j : M + j + 1], scale=1.0,
+                )
+            nc.scalar.copy(out=cb_all[n][:, :, first + 1 : first + 1 + GROUP], in_=cb[:])
+
+            z = z_all[n][:, :, first : first + GROUP]
+            max4 = work.tile([P, 4, GROUP], F32)
+            nc.vector.tensor_tensor(out=max4[:], in0=z[:, 0:4, :], in1=z[:, 4:8, :], op=ALU.max)
+            max2 = work.tile([P, 2, GROUP], F32)
+            nc.vector.tensor_tensor(out=max2[:], in0=max4[:, 0:2, :], in1=max4[:, 2:4, :], op=ALU.max)
+            max1 = work.tile([P, 1, GROUP], F32)
+            nc.vector.tensor_tensor(out=max1[:], in0=max2[:, 0:1, :], in1=max2[:, 1:2, :], op=ALU.max)
+
+            terms = work.tile([P, 2, 2 * M, GROUP], F32)
+            for s in range(2):
+                ks = slice(M * s, M * (s + 1))
+                nc.vector.tensor_tensor(
+                    out=terms[:, 0, ks, :], in0=z[:, ks, :], in1=max1.to_broadcast([P, M, GROUP]), op=ALU.subtract
+                )
+                nc.scalar.activation(out=terms[:, 0, ks, :], in_=terms[:, 0, ks, :], func=ACT.Exp)
+            nc.vector.tensor_tensor(out=terms[:, 1, 0:M, :], in0=terms[:, 0, 0:M, :], in1=ca[:], op=ALU.mult)
+            nc.vector.tensor_tensor(
+                out=terms[:, 1, M : 2 * M, :], in0=terms[:, 0, M : 2 * M, :],
+                in1=cb_all[n][:, :, first : first + GROUP], op=ALU.mult,
+            )
+            sum4 = work.tile([P, 2, 4, GROUP], F32)
+            nc.vector.tensor_tensor(out=sum4[:], in0=terms[:, :, 0:4, :], in1=terms[:, :, 4:8, :], op=ALU.add)
+            sum2 = work.tile([P, 2, 2, GROUP], F32)
+            nc.vector.tensor_tensor(out=sum2[:], in0=sum4[:, :, 0:2, :], in1=sum4[:, :, 2:4, :], op=ALU.add)
+            nc.vector.tensor_tensor(
+                out=sums[:, :, GROUP * g : GROUP * (g + 1)], in0=sum2[:, :, 0, :], in1=sum2[:, :, 1, :], op=ALU.add
+            )
+
+        rsqrt = keep.tile([P, GROUPS * GROUP], F32)
+        nc.scalar.activation(out=rsqrt[:], in_=sums[:, 0, :], func=ACT.Abs_reciprocal_sqrt)
+        recip = keep.tile([P, GROUPS * GROUP], F32)
+        nc.scalar.activation(out=recip[:], in_=rsqrt[:], func=ACT.Square)
+        result = keep.tile([P, GROUPS * GROUP], F32)
+        nc.vector.tensor_tensor(out=result[:], in0=sums[:, 1, :], in1=recip[:], op=ALU.mult)
+        result_ps = psum.tile([P, GROUPS, CH], F32, tag="tp")
+        for g in range(GROUPS):
+            nc.tensor.transpose(
+                out=result_ps[:, g, :], in_=result[:, GROUP * g : GROUP * (g + 1)], identity=ident[:]
+            )
+        result_rows = keep.tile([P, GROUPS, CH], F32)
+        nc.vector.tensor_copy(out=result_rows[:], in_=result_ps[:])
+        nc.sync.dma_start(out=out_rows, in_=result_rows[:])

@@ -24,6 +24,7 @@ GROUPS = BATCH * TOKENS // (M * GROUP)
 GROUPS_PER_BATCH = GROUPS // BATCH
 BLOCKS = TOKENS // M
 NEG = -1e30
+ZA, ZB, CA, CB = 0, 1, 2, 3
 
 FLOPS = 2 * BATCH * TOKENS * D * 4 * CH
 
@@ -38,37 +39,25 @@ def tile_tokencompressor_pa_kernel(tc, H, W_a_KV, W_b_KV, W_a_Z, W_b_Z, B_a, B_b
         keep = stack.enter_context(tc.tile_pool(name="keep", bufs=1))
         work = stack.enter_context(tc.tile_pool(name="work", bufs=2))
         psum = stack.enter_context(tc.psum_pool(name="psum", bufs=1))
+        stack.enter_context(tc.manual_schedule())
 
         h_raw = [keep.tile([P, M, D], BF16, name="h_raw%d" % g) for g in range(GROUPS)]
         w_raw = keep.tile([P, 4, PASSES, 4, CH], BF16)
-
-        def load_h(g):
-            for half in range(2):
-                js = slice(2 * half, 2 * half + 2)
-                nc.sync.dma_start(out=h_raw[g][:, js, :], in_=h_groups[g][:, js, :])
-
-        load_h(0)
+        bias_rows = keep.tile([P, P], BF16)
+        nc.vector.memset(bias_rows[:], 0.0)
+        nc.scalar.dma_start(out=bias_rows[0:M, :], in_=B_a)
+        nc.scalar.dma_start(out=bias_rows[M : 2 * M, :], in_=B_b)
+        nc.sync.dma_start(out=h_raw[0][:], in_=h_groups[0])
         for w in range(4):
             nc.sync.dma_start(
                 out=w_raw[:, w].rearrange("p c (u e) n -> p c u e n", e=2),
                 in_=weights[w].rearrange("(c u p e) n -> p c u e n", c=PASSES, u=2, e=2),
             )
         for g in range(1, GROUPS):
-            load_h(g)
+            nc.sync.dma_start(out=h_raw[g][:], in_=h_groups[g])
 
         ident = keep.tile([P, P], F32)
         make_identity(nc, ident[:])
-
-        bias_rows = keep.tile([P, P], BF16)
-        nc.vector.memset(bias_rows[:], 0.0)
-        nc.scalar.dma_start(out=bias_rows[0:M, :], in_=B_a)
-        nc.scalar.dma_start(out=bias_rows[M : 2 * M, :], in_=B_b)
-        bias_rows32 = keep.tile([P, P], F32)
-        nc.vector.tensor_copy(out=bias_rows32[:], in_=bias_rows[:])
-        bias_ps = psum.tile([P, P], F32, tag="tp")
-        nc.tensor.transpose(out=bias_ps[:], in_=bias_rows32[:], identity=ident[:])
-        bias = keep.tile([P, 2 * M], F32)
-        nc.vector.tensor_copy(out=bias[:], in_=bias_ps[:, 0 : 2 * M])
 
         z_all = [keep.tile([P, 2 * M, BLOCKS + 1], F32, name="z_all%d" % n) for n in range(BATCH)]
         cb_all = [keep.tile([P, M, BLOCKS + 1], F32, name="cb_all%d" % n) for n in range(BATCH)]
@@ -77,27 +66,40 @@ def tile_tokencompressor_pa_kernel(tc, H, W_a_KV, W_b_KV, W_a_Z, W_b_Z, B_a, B_b
             nc.vector.memset(cb_all[n][:, :, 0:1], 0.0)
         sums = keep.tile([P, 2, GROUPS * GROUP], F32)
 
+        bias_rows32 = keep.tile([P, P], F32)
+        nc.vector.tensor_copy(out=bias_rows32[:], in_=bias_rows[:])
+        bias_ps = psum.tile([P, P], F32, tag="xt", bufs=4)
+        nc.tensor.transpose(out=bias_ps[:], in_=bias_rows32[:], identity=ident[:])
+        bias = keep.tile([P, 2 * M], F32)
+        nc.vector.tensor_copy(out=bias[:], in_=bias_ps[:, 0 : 2 * M])
+
         w_grouped = keep.tile([P, 4, PASSES, CH, 4], BF16, align_bytes=64)
         w_codes = keep.tile([P, 4, PASSES, CH], U32, align_bytes=64)
         w_scales = keep.tile([P, 4, PASSES, CH], U8, align_bytes=64)
-        for w in range(4):
+
+        def regroup_w(w):
             nc.vector.tensor_copy(out=w_grouped[:, w], in_=w_raw[:, w].rearrange("p c t n -> p c n t"))
-        for w in range(4):
+
+        def quantise_w(w):
             nc.vector.quantize_mx(
                 out=w_codes[:, w].rearrange("p c n -> p (c n)").bitcast(FP8X4),
                 scales=w_scales[:, w].rearrange("p c n -> p (c n)"),
                 in_=w_grouped[:, w].rearrange("p c n t -> p (c n t)"),
             )
 
-        def quantise_h(g):
+        h_grouped = {}
+        h_codes = {}
+        h_scales = {}
+        acc = {}
+        max4, max2, max1, terms, sum4, sum2 = {}, {}, {}, {}, {}, {}
+
+        def transpose_h(g):
             h_words = h_raw[g].bitcast(F32)
-            h_grouped = work.tile([P, PASSES, M * GROUP, 4], BF16, align_bytes=64)
-            h_grouped_words = h_grouped.bitcast(F32)
-            h_codes = work.tile([P, PASSES, M * GROUP], U32, align_bytes=64)
-            h_scales = work.tile([P, PASSES, M * GROUP], U8, align_bytes=64)
+            h_grouped[g] = work.tile([P, PASSES, M * GROUP, 4], BF16, align_bytes=64, name="h_grouped", tag="h_grouped")
+            h_grouped_words = h_grouped[g].bitcast(F32)
             for c in range(PASSES):
                 for half in range(2):
-                    xt = psum.tile([P, 2, 2, GROUP], F32, tag="xt", bufs=3)
+                    xt = psum.tile([P, 2, 2, GROUP], F32, tag="xt", bufs=4)
                     for u in range(2):
                         for jj in range(2):
                             first = 256 * c + 128 * u
@@ -111,90 +113,174 @@ def tile_tokencompressor_pa_kernel(tc, H, W_a_KV, W_b_KV, W_a_Z, W_b_Z, B_a, B_b
                         out=h_grouped_words[:, c, cols, :],
                         in_=xt.rearrange("p u jj i -> p (jj i) u"),
                     )
-                nc.vector.quantize_mx(
-                    out=h_codes[:, c, :].bitcast(FP8X4),
-                    scales=h_scales[:, c, :],
-                    in_=h_grouped[:, c].rearrange("p col t -> p (col t)"),
-                )
-            return h_codes, h_scales
 
-        def project(w, h_codes, h_scales, tag):
-            acc = psum.tile([P, M, GROUP], F32, tag=tag)
-            for c in range(PASSES):
-                nc.tensor.matmul_mx(
-                    out=acc.rearrange("p j i -> p (j i)"),
-                    lhsT=w_codes[:, w, c, :].bitcast(FP8X4),
-                    lhsT_scale=w_scales[:, w, c, :],
-                    rhs=h_codes[:, c, :].bitcast(FP8X4),
-                    rhs_scale=h_scales[:, c, :],
-                    start=(c == 0),
-                    stop=(c == PASSES - 1),
-                )
-            return acc
-
-        quantised = quantise_h(0)
-        for g in range(GROUPS):
-            n = g // GROUPS_PER_BATCH
-            first = GROUP * (g % GROUPS_PER_BATCH)
-            h_codes, h_scales = quantised
-            za = project(0, h_codes, h_scales, "za")
-            zb = project(1, h_codes, h_scales, "zb")
-            ca = project(2, h_codes, h_scales, "ca")
-            cb = project(3, h_codes, h_scales, "cb")
-            if g + 1 < GROUPS:
-                quantised = quantise_h(g + 1)
-
-            for j in range(M):
-                nc.scalar.activation(
-                    out=z_all[n][:, j, first : first + GROUP], in_=za[:, j, :],
-                    func=ACT.Identity, bias=bias[:, j : j + 1], scale=1.0,
-                )
-            for j in range(M):
-                nc.scalar.activation(
-                    out=z_all[n][:, M + j, first + 1 : first + 1 + GROUP], in_=zb[:, j, :],
-                    func=ACT.Identity, bias=bias[:, M + j : M + j + 1], scale=1.0,
-                )
-            nc.scalar.copy(out=cb_all[n][:, :, first + 1 : first + 1 + GROUP], in_=cb[:])
-
-            z = z_all[n][:, :, first : first + GROUP]
-            max4 = work.tile([P, 4, GROUP], F32)
-            nc.vector.tensor_tensor(out=max4[:], in0=z[:, 0:4, :], in1=z[:, 4:8, :], op=ALU.max)
-            max2 = work.tile([P, 2, GROUP], F32)
-            nc.vector.tensor_tensor(out=max2[:], in0=max4[:, 0:2, :], in1=max4[:, 2:4, :], op=ALU.max)
-            max1 = work.tile([P, 1, GROUP], F32)
-            nc.vector.tensor_tensor(out=max1[:], in0=max2[:, 0:1, :], in1=max2[:, 1:2, :], op=ALU.max)
-
-            terms = work.tile([P, 2, 2 * M, GROUP], F32)
-            for s in range(2):
-                ks = slice(M * s, M * (s + 1))
-                nc.vector.tensor_tensor(
-                    out=terms[:, 0, ks, :], in0=z[:, ks, :], in1=max1.to_broadcast([P, M, GROUP]), op=ALU.subtract
-                )
-                nc.scalar.activation(out=terms[:, 0, ks, :], in_=terms[:, 0, ks, :], func=ACT.Exp)
-            nc.vector.tensor_tensor(out=terms[:, 1, 0:M, :], in0=terms[:, 0, 0:M, :], in1=ca[:], op=ALU.mult)
-            nc.vector.tensor_tensor(
-                out=terms[:, 1, M : 2 * M, :], in0=terms[:, 0, M : 2 * M, :],
-                in1=cb_all[n][:, :, first : first + GROUP], op=ALU.mult,
+        def quantise_h(g, c):
+            if c == 0:
+                h_codes[g] = work.tile([P, PASSES, M * GROUP], U32, align_bytes=64, name="h_codes", tag="h_codes")
+                h_scales[g] = work.tile([P, PASSES, M * GROUP], U8, align_bytes=64, name="h_scales", tag="h_scales")
+            nc.vector.quantize_mx(
+                out=h_codes[g][:, c, :].bitcast(FP8X4),
+                scales=h_scales[g][:, c, :],
+                in_=h_grouped[g][:, c].rearrange("p col t -> p (col t)"),
             )
-            sum4 = work.tile([P, 2, 4, GROUP], F32)
-            nc.vector.tensor_tensor(out=sum4[:], in0=terms[:, :, 0:4, :], in1=terms[:, :, 4:8, :], op=ALU.add)
-            sum2 = work.tile([P, 2, 2, GROUP], F32)
-            nc.vector.tensor_tensor(out=sum2[:], in0=sum4[:, :, 0:2, :], in1=sum4[:, :, 2:4, :], op=ALU.add)
+
+        def project(g, w, c):
+            if c == 0:
+                acc[g, w] = psum.tile([P, M, GROUP], F32, name="acc%d" % w, tag="acc%d" % w)
+            nc.tensor.matmul_mx(
+                out=acc[g, w].rearrange("p j i -> p (j i)"),
+                lhsT=w_codes[:, w, c, :].bitcast(FP8X4),
+                lhsT_scale=w_scales[:, w, c, :],
+                rhs=h_codes[g][:, c, :].bitcast(FP8X4),
+                rhs_scale=h_scales[g][:, c, :],
+                start=(c == 0),
+                stop=(c == PASSES - 1),
+            )
+
+        def place(g):
+            return g // GROUPS_PER_BATCH, GROUP * (g % GROUPS_PER_BATCH)
+
+        def add_bias(g, s):
+            n, first = place(g)
+            for j in range(M):
+                k = M * s + j
+                nc.scalar.activation(
+                    out=z_all[n][:, k, first + s : first + s + GROUP], in_=acc[g, ZA + s][:, j, :],
+                    func=ACT.Identity, bias=bias[:, k : k + 1], scale=1.0,
+                )
+
+        def copy_cb(g):
+            n, first = place(g)
+            nc.scalar.copy(out=cb_all[n][:, :, first + 1 : first + 1 + GROUP], in_=acc[g, CB][:])
+
+        def logits(g):
+            n, first = place(g)
+            return z_all[n][:, :, first : first + GROUP]
+
+        def max_of_8(g):
+            max4[g] = work.tile([P, 4, GROUP], F32, name="max4", tag="max4")
+            nc.vector.tensor_tensor(out=max4[g][:], in0=logits(g)[:, 0:4, :], in1=logits(g)[:, 4:8, :], op=ALU.max)
+
+        def max_of_4(g):
+            max2[g] = work.tile([P, 2, GROUP], F32, name="max2", tag="max2")
+            nc.vector.tensor_tensor(out=max2[g][:], in0=max4[g][:, 0:2, :], in1=max4[g][:, 2:4, :], op=ALU.max)
+
+        def max_of_2(g):
+            max1[g] = work.tile([P, 1, GROUP], F32, name="max1", tag="max1")
+            nc.vector.tensor_tensor(out=max1[g][:], in0=max2[g][:, 0:1, :], in1=max2[g][:, 1:2, :], op=ALU.max)
+
+        def exponentials(g, s):
+            if s == 0:
+                terms[g] = work.tile([P, 2, 2 * M, GROUP], F32, name="terms", tag="terms")
+            ks = slice(M * s, M * (s + 1))
             nc.vector.tensor_tensor(
-                out=sums[:, :, GROUP * g : GROUP * (g + 1)], in0=sum2[:, :, 0, :], in1=sum2[:, :, 1, :], op=ALU.add
+                out=terms[g][:, 0, ks, :], in0=logits(g)[:, ks, :],
+                in1=max1[g].to_broadcast([P, M, GROUP]), op=ALU.subtract,
+            )
+            nc.scalar.activation(out=terms[g][:, 0, ks, :], in_=terms[g][:, 0, ks, :], func=ACT.Exp)
+
+        def times_values(g, s):
+            n, first = place(g)
+            ks = slice(M * s, M * (s + 1))
+            values = acc[g, CA][:] if s == 0 else cb_all[n][:, :, first : first + GROUP]
+            nc.vector.tensor_tensor(out=terms[g][:, 1, ks, :], in0=terms[g][:, 0, ks, :], in1=values, op=ALU.mult)
+
+        def sum_of_8(g):
+            sum4[g] = work.tile([P, 2, 4, GROUP], F32, name="sum4", tag="sum4")
+            nc.vector.tensor_tensor(out=sum4[g][:], in0=terms[g][:, :, 0:4, :], in1=terms[g][:, :, 4:8, :], op=ALU.add)
+
+        def sum_of_4(g):
+            sum2[g] = work.tile([P, 2, 2, GROUP], F32, name="sum2", tag="sum2")
+            nc.vector.tensor_tensor(out=sum2[g][:], in0=sum4[g][:, :, 0:2, :], in1=sum4[g][:, :, 2:4, :], op=ALU.add)
+
+        def sum_of_2(g):
+            nc.vector.tensor_tensor(
+                out=sums[:, :, GROUP * g : GROUP * (g + 1)], in0=sum2[g][:, :, 0, :], in1=sum2[g][:, :, 1, :],
+                op=ALU.add,
             )
 
         rsqrt = keep.tile([P, GROUPS * GROUP], F32)
-        nc.scalar.activation(out=rsqrt[:], in_=sums[:, 0, :], func=ACT.Abs_reciprocal_sqrt)
         recip = keep.tile([P, GROUPS * GROUP], F32)
-        nc.scalar.activation(out=recip[:], in_=rsqrt[:], func=ACT.Square)
         result = keep.tile([P, GROUPS * GROUP], F32)
-        nc.vector.tensor_tensor(out=result[:], in0=sums[:, 1, :], in1=recip[:], op=ALU.mult)
-        result_ps = psum.tile([P, GROUPS, CH], F32, tag="tp")
-        for g in range(GROUPS):
-            nc.tensor.transpose(
-                out=result_ps[:, g, :], in_=result[:, GROUP * g : GROUP * (g + 1)], identity=ident[:]
-            )
         result_rows = keep.tile([P, GROUPS, CH], F32)
-        nc.vector.tensor_copy(out=result_rows[:], in_=result_ps[:])
-        nc.sync.dma_start(out=out_rows, in_=result_rows[:])
+
+        def reciprocal_of_sum(g0, g1):
+            cols = slice(GROUP * g0, GROUP * g1)
+            nc.scalar.activation(out=rsqrt[:, cols], in_=sums[:, 0, cols], func=ACT.Abs_reciprocal_sqrt)
+            nc.scalar.activation(out=recip[:, cols], in_=rsqrt[:, cols], func=ACT.Square)
+
+        def finish(g0, g1):
+            cols = slice(GROUP * g0, GROUP * g1)
+            nc.vector.tensor_tensor(out=result[:, cols], in0=sums[:, 1, cols], in1=recip[:, cols], op=ALU.mult)
+            result_ps = psum.tile([P, g1 - g0, CH], F32, tag="xt", bufs=4)
+            for g in range(g0, g1):
+                nc.tensor.transpose(
+                    out=result_ps[:, g - g0, :], in_=result[:, GROUP * g : GROUP * (g + 1)], identity=ident[:]
+                )
+            nc.scalar.copy(out=result_rows[:, g0:g1, :], in_=result_ps[:])
+            nc.sync.dma_start(out=out_rows[:, g0:g1, :], in_=result_rows[:, g0:g1, :])
+
+        transpose_h(0)
+        regroup_w(ZA)
+        quantise_h(0, 0)
+        quantise_w(ZA)
+        regroup_w(ZB)
+        quantise_h(0, 1)
+        quantise_w(ZB)
+        for s in range(2):
+            for c in range(PASSES):
+                project(0, ZA + s, c)
+            add_bias(0, s)
+        regroup_w(CA)
+        regroup_w(CB)
+        quantise_w(CA)
+        quantise_w(CB)
+        transpose_h(1)
+        for w in (CB, CA):
+            for c in range(PASSES):
+                project(0, w, c)
+        copy_cb(0)
+
+        for g in range(GROUPS):
+            ahead = g + 1 < GROUPS
+            max_of_8(g)
+            if ahead:
+                quantise_h(g + 1, 0)
+                project(g + 1, ZA, 0)
+                project(g + 1, ZB, 0)
+            max_of_4(g)
+            if ahead:
+                quantise_h(g + 1, 1)
+                project(g + 1, ZA, 1)
+                project(g + 1, ZB, 1)
+                add_bias(g + 1, 0)
+                add_bias(g + 1, 1)
+            max_of_2(g)
+            if g > 0:
+                sum_of_8(g - 1)
+            exponentials(g, 0)
+            if g > 0:
+                sum_of_4(g - 1)
+            exponentials(g, 1)
+            if g > 0:
+                sum_of_2(g - 1)
+            if g + 2 < GROUPS:
+                transpose_h(g + 2)
+            if ahead:
+                project(g + 1, CB, 0)
+                project(g + 1, CB, 1)
+                copy_cb(g + 1)
+            times_values(g, 0)
+            if ahead:
+                project(g + 1, CA, 0)
+                project(g + 1, CA, 1)
+            times_values(g, 1)
+
+        last = GROUPS - 1
+        reciprocal_of_sum(0, last)
+        sum_of_8(last)
+        sum_of_4(last)
+        sum_of_2(last)
+        reciprocal_of_sum(last, GROUPS)
+        finish(0, last)
+        finish(last, GROUPS)

@@ -64,11 +64,12 @@ def tile_tokencompressor_pa_kernel(tc, H, W_a_KV, W_b_KV, W_a_Z, W_b_Z, B_a, B_b
         for n in range(BATCH):
             nc.vector.memset(z_all[n][:, M : 2 * M, 0:1], NEG)
             nc.vector.memset(cb_all[n][:, :, 0:1], 0.0)
-        sums = keep.tile([P, 2, GROUPS * GROUP], F32)
+        den_ps = psum.tile([P, GROUPS, CH], F32)
+        num_ps = psum.tile([P, GROUPS, CH], F32)
 
         bias_rows32 = keep.tile([P, P], F32)
         nc.vector.tensor_copy(out=bias_rows32[:], in_=bias_rows[:])
-        bias_ps = psum.tile([P, P], F32, tag="xt", bufs=4)
+        bias_ps = psum.tile([P, P], F32, tag="xt", bufs=2)
         nc.tensor.transpose(out=bias_ps[:], in_=bias_rows32[:], identity=ident[:])
         bias = keep.tile([P, 2 * M], F32)
         nc.vector.tensor_copy(out=bias[:], in_=bias_ps[:, 0 : 2 * M])
@@ -91,28 +92,32 @@ def tile_tokencompressor_pa_kernel(tc, H, W_a_KV, W_b_KV, W_a_Z, W_b_Z, B_a, B_b
         h_codes = {}
         h_scales = {}
         acc = {}
-        max4, max2, max1, terms, sum4, sum2 = {}, {}, {}, {}, {}, {}
+        xt = {}
+        max4, max2, max1, terms = {}, {}, {}, {}
 
-        def transpose_h(g):
+        def transposes(g, c):
             h_words = h_raw[g].bitcast(F32)
-            h_grouped[g] = work.tile([P, PASSES, M * GROUP, 4], BF16, align_bytes=64, name="h_grouped", tag="h_grouped")
+            for half in range(2):
+                xt[g, c, half] = psum.tile([P, 2, 2, GROUP], F32, name="xt", tag="xt", bufs=2)
+                for u in range(2):
+                    for jj in range(2):
+                        first = 256 * c + 128 * u
+                        nc.tensor.transpose(
+                            out=xt[g, c, half][:, u, jj, :],
+                            in_=h_words[:, 2 * half + jj, first : first + 128],
+                            identity=ident[:],
+                        )
+
+        def copies(g, c):
+            if c == 0:
+                h_grouped[g] = work.tile([P, PASSES, M * GROUP, 4], BF16, align_bytes=64, name="h_grouped", tag="h_grouped")
             h_grouped_words = h_grouped[g].bitcast(F32)
-            for c in range(PASSES):
-                for half in range(2):
-                    xt = psum.tile([P, 2, 2, GROUP], F32, tag="xt", bufs=4)
-                    for u in range(2):
-                        for jj in range(2):
-                            first = 256 * c + 128 * u
-                            nc.tensor.transpose(
-                                out=xt[:, u, jj, :],
-                                in_=h_words[:, 2 * half + jj, first : first + 128],
-                                identity=ident[:],
-                            )
-                    cols = slice(2 * GROUP * half, 2 * GROUP * (half + 1))
-                    nc.scalar.copy(
-                        out=h_grouped_words[:, c, cols, :],
-                        in_=xt.rearrange("p u jj i -> p (jj i) u"),
-                    )
+            for half in range(2):
+                cols = slice(2 * GROUP * half, 2 * GROUP * (half + 1))
+                nc.scalar.copy(
+                    out=h_grouped_words[:, c, cols, :],
+                    in_=xt[g, c, half].rearrange("p u jj i -> p (jj i) u"),
+                )
 
         def quantise_h(g, c):
             if c == 0:
@@ -169,7 +174,7 @@ def tile_tokencompressor_pa_kernel(tc, H, W_a_KV, W_b_KV, W_a_Z, W_b_Z, B_a, B_b
             max1[g] = work.tile([P, 1, GROUP], F32, name="max1", tag="max1")
             nc.vector.tensor_tensor(out=max1[g][:], in0=max2[g][:, 0:1, :], in1=max2[g][:, 1:2, :], op=ALU.max)
 
-        def exponentials(g, s):
+        def subtract_max(g, s):
             if s == 0:
                 terms[g] = work.tile([P, 2, 2 * M, GROUP], F32, name="terms", tag="terms")
             ks = slice(M * s, M * (s + 1))
@@ -177,6 +182,9 @@ def tile_tokencompressor_pa_kernel(tc, H, W_a_KV, W_b_KV, W_a_Z, W_b_Z, B_a, B_b
                 out=terms[g][:, 0, ks, :], in0=logits(g)[:, ks, :],
                 in1=max1[g].to_broadcast([P, M, GROUP]), op=ALU.subtract,
             )
+
+        def exponentials(g, s):
+            ks = slice(M * s, M * (s + 1))
             nc.scalar.activation(out=terms[g][:, 0, ks, :], in_=terms[g][:, 0, ks, :], func=ACT.Exp)
 
         def times_values(g, s):
@@ -185,42 +193,30 @@ def tile_tokencompressor_pa_kernel(tc, H, W_a_KV, W_b_KV, W_a_Z, W_b_Z, B_a, B_b
             values = acc[g, CA][:] if s == 0 else cb_all[n][:, :, first : first + GROUP]
             nc.vector.tensor_tensor(out=terms[g][:, 1, ks, :], in0=terms[g][:, 0, ks, :], in1=values, op=ALU.mult)
 
-        def sum_of_8(g):
-            sum4[g] = work.tile([P, 2, 4, GROUP], F32, name="sum4", tag="sum4")
-            nc.vector.tensor_tensor(out=sum4[g][:], in0=terms[g][:, :, 0:4, :], in1=terms[g][:, :, 4:8, :], op=ALU.add)
+        def sum_and_turn(g, q, total):
+            for k in range(2 * M):
+                nc.tensor.matmul(
+                    out=total[:, g, :], lhsT=terms[g][:, q, k, :], rhs=ident[:], is_transpose=True,
+                    start=(k == 0), stop=(k == 2 * M - 1),
+                )
 
-        def sum_of_4(g):
-            sum2[g] = work.tile([P, 2, 2, GROUP], F32, name="sum2", tag="sum2")
-            nc.vector.tensor_tensor(out=sum2[g][:], in0=sum4[g][:, :, 0:2, :], in1=sum4[g][:, :, 2:4, :], op=ALU.add)
-
-        def sum_of_2(g):
-            nc.vector.tensor_tensor(
-                out=sums[:, :, GROUP * g : GROUP * (g + 1)], in0=sum2[g][:, :, 0, :], in1=sum2[g][:, :, 1, :],
-                op=ALU.add,
-            )
-
-        rsqrt = keep.tile([P, GROUPS * GROUP], F32)
-        recip = keep.tile([P, GROUPS * GROUP], F32)
-        result = keep.tile([P, GROUPS * GROUP], F32)
+        rsqrt = keep.tile([P, GROUPS, CH], F32)
+        recip = keep.tile([P, GROUPS, CH], F32)
         result_rows = keep.tile([P, GROUPS, CH], F32)
 
         def reciprocal_of_sum(g0, g1):
-            cols = slice(GROUP * g0, GROUP * g1)
-            nc.scalar.activation(out=rsqrt[:, cols], in_=sums[:, 0, cols], func=ACT.Abs_reciprocal_sqrt)
-            nc.scalar.activation(out=recip[:, cols], in_=rsqrt[:, cols], func=ACT.Square)
+            nc.scalar.activation(out=rsqrt[:, g0:g1, :], in_=den_ps[:, g0:g1, :], func=ACT.Abs_reciprocal_sqrt)
+            nc.scalar.activation(out=recip[:, g0:g1, :], in_=rsqrt[:, g0:g1, :], func=ACT.Square)
 
         def finish(g0, g1):
-            cols = slice(GROUP * g0, GROUP * g1)
-            nc.vector.tensor_tensor(out=result[:, cols], in0=sums[:, 1, cols], in1=recip[:, cols], op=ALU.mult)
-            result_ps = psum.tile([P, g1 - g0, CH], F32, tag="xt", bufs=4)
-            for g in range(g0, g1):
-                nc.tensor.transpose(
-                    out=result_ps[:, g - g0, :], in_=result[:, GROUP * g : GROUP * (g + 1)], identity=ident[:]
-                )
-            nc.scalar.copy(out=result_rows[:, g0:g1, :], in_=result_ps[:])
+            nc.vector.tensor_tensor(
+                out=result_rows[:, g0:g1, :], in0=num_ps[:, g0:g1, :], in1=recip[:, g0:g1, :], op=ALU.mult
+            )
             nc.sync.dma_start(out=out_rows[:, g0:g1, :], in_=result_rows[:, g0:g1, :])
 
-        transpose_h(0)
+        for c in range(PASSES):
+            transposes(0, c)
+            copies(0, c)
         regroup_w(ZA)
         quantise_h(0, 0)
         quantise_w(ZA)
@@ -231,56 +227,54 @@ def tile_tokencompressor_pa_kernel(tc, H, W_a_KV, W_b_KV, W_a_Z, W_b_Z, B_a, B_b
             for c in range(PASSES):
                 project(0, ZA + s, c)
             add_bias(0, s)
-        regroup_w(CA)
         regroup_w(CB)
-        quantise_w(CA)
+        regroup_w(CA)
         quantise_w(CB)
-        transpose_h(1)
+        quantise_w(CA)
+        transposes(1, 0)
         for w in (CB, CA):
             for c in range(PASSES):
                 project(0, w, c)
-        copy_cb(0)
 
         for g in range(GROUPS):
             ahead = g + 1 < GROUPS
+            if ahead:
+                copies(g + 1, 0)
+                transposes(g + 1, 1)
+                copies(g + 1, 1)
             max_of_8(g)
+            max_of_4(g)
+            max_of_2(g)
             if ahead:
                 quantise_h(g + 1, 0)
                 project(g + 1, ZA, 0)
                 project(g + 1, ZB, 0)
-            max_of_4(g)
+            subtract_max(g, 0)
             if ahead:
                 quantise_h(g + 1, 1)
                 project(g + 1, ZA, 1)
                 project(g + 1, ZB, 1)
+            subtract_max(g, 1)
+            copy_cb(g)
+            exponentials(g, 0)
+            exponentials(g, 1)
+            if ahead:
                 add_bias(g + 1, 0)
                 add_bias(g + 1, 1)
-            max_of_2(g)
-            if g > 0:
-                sum_of_8(g - 1)
-            exponentials(g, 0)
-            if g > 0:
-                sum_of_4(g - 1)
-            exponentials(g, 1)
-            if g > 0:
-                sum_of_2(g - 1)
-            if g + 2 < GROUPS:
-                transpose_h(g + 2)
-            if ahead:
                 project(g + 1, CB, 0)
                 project(g + 1, CB, 1)
-                copy_cb(g + 1)
+            sum_and_turn(g, 0, den_ps)
+            if g + 2 < GROUPS:
+                transposes(g + 2, 0)
             times_values(g, 0)
             if ahead:
                 project(g + 1, CA, 0)
                 project(g + 1, CA, 1)
             times_values(g, 1)
+            sum_and_turn(g, 1, num_ps)
 
         last = GROUPS - 1
         reciprocal_of_sum(0, last)
-        sum_of_8(last)
-        sum_of_4(last)
-        sum_of_2(last)
         reciprocal_of_sum(last, GROUPS)
         finish(0, last)
         finish(last, GROUPS)

@@ -23,6 +23,9 @@ GROUP = 128
 GROUPS = BATCH * TOKENS // (M * GROUP)
 GROUPS_PER_BATCH = GROUPS // BATCH
 BLOCKS = TOKENS // M
+HALF = M // 2
+UNITS = 2 * GROUPS
+UNIT_COLS = HALF * GROUP
 NEG = -1e30
 ZA, ZB, CA, CB = 0, 1, 2, 3
 
@@ -44,17 +47,28 @@ def tile_tokencompressor_pa_kernel(tc, H, W_a_KV, W_b_KV, W_a_Z, W_b_Z, B_a, B_b
         h_raw = [keep.tile([P, M, D], BF16, name="h_raw%d" % g) for g in range(GROUPS)]
         w_raw = keep.tile([P, 4, PASSES, 4, CH], BF16)
         bias_rows = keep.tile([P, P], BF16)
-        nc.vector.memset(bias_rows[:], 0.0)
-        nc.scalar.dma_start(out=bias_rows[0:M, :], in_=B_a)
-        nc.scalar.dma_start(out=bias_rows[M : 2 * M, :], in_=B_b)
-        nc.sync.dma_start(out=h_raw[0][:], in_=h_groups[0])
-        for w in range(4):
+
+        def load_h(u):
+            js = slice(HALF * (u % 2), HALF * (u % 2 + 1))
+            nc.sync.dma_start(out=h_raw[u // 2][:, js, :], in_=h_groups[u // 2][:, js, :])
+
+        def load_w(w):
             nc.sync.dma_start(
                 out=w_raw[:, w].rearrange("p c (u e) n -> p c u e n", e=2),
                 in_=weights[w].rearrange("(c u p e) n -> p c u e n", c=PASSES, u=2, e=2),
             )
-        for g in range(1, GROUPS):
-            nc.sync.dma_start(out=h_raw[g][:], in_=h_groups[g])
+
+        nc.vector.memset(bias_rows[:], 0.0)
+        nc.sync.dma_start(out=bias_rows[0:M, :], in_=B_a)
+        nc.sync.dma_start(out=bias_rows[M : 2 * M, :], in_=B_b)
+        load_h(0)
+        load_w(ZA)
+        load_w(ZB)
+        load_h(1)
+        load_w(CB)
+        load_w(CA)
+        for u in range(2, UNITS):
+            load_h(u)
 
         ident = keep.tile([P, P], F32)
         make_identity(nc, ident[:])
@@ -69,7 +83,7 @@ def tile_tokencompressor_pa_kernel(tc, H, W_a_KV, W_b_KV, W_a_Z, W_b_Z, B_a, B_b
 
         bias_rows32 = keep.tile([P, P], F32)
         nc.vector.tensor_copy(out=bias_rows32[:], in_=bias_rows[:])
-        bias_ps = psum.tile([P, P], F32, tag="xt", bufs=2)
+        bias_ps = psum.tile([P, P], F32, tag="ca")
         nc.tensor.transpose(out=bias_ps[:], in_=bias_rows32[:], identity=ident[:])
         bias = keep.tile([P, 2 * M], F32)
         nc.vector.tensor_copy(out=bias[:], in_=bias_ps[:, 0 : 2 * M])
@@ -88,89 +102,91 @@ def tile_tokencompressor_pa_kernel(tc, H, W_a_KV, W_b_KV, W_a_Z, W_b_Z, B_a, B_b
                 in_=w_grouped[:, w].rearrange("p c n t -> p (c n t)"),
             )
 
-        h_grouped = {}
-        h_codes = {}
-        h_scales = {}
-        acc = {}
-        xt = {}
+        xt, h_grouped, h_codes, h_scales = {}, {}, {}, {}
+        z_ps, cb_ps, ca_ps = {}, {}, {}
         max4, max2, max1, terms = {}, {}, {}, {}
 
-        def transposes(g, c):
-            h_words = h_raw[g].bitcast(F32)
-            for half in range(2):
-                xt[g, c, half] = psum.tile([P, 2, 2, GROUP], F32, name="xt", tag="xt", bufs=2)
-                for u in range(2):
-                    for jj in range(2):
-                        first = 256 * c + 128 * u
+        def transposes(u):
+            h_words = h_raw[u // 2].bitcast(F32)
+            for c in range(PASSES):
+                xt[u, c] = psum.tile([P, 2, HALF, GROUP], F32, name="xt", tag="xt", bufs=2)
+                for v in range(2):
+                    for jj in range(HALF):
+                        first = 256 * c + 128 * v
                         nc.tensor.transpose(
-                            out=xt[g, c, half][:, u, jj, :],
-                            in_=h_words[:, 2 * half + jj, first : first + 128],
+                            out=xt[u, c][:, v, jj, :],
+                            in_=h_words[:, HALF * (u % 2) + jj, first : first + 128],
                             identity=ident[:],
                         )
 
-        def copies(g, c):
-            if c == 0:
-                h_grouped[g] = work.tile([P, PASSES, M * GROUP, 4], BF16, align_bytes=64, name="h_grouped", tag="h_grouped")
-            h_grouped_words = h_grouped[g].bitcast(F32)
-            for half in range(2):
-                cols = slice(2 * GROUP * half, 2 * GROUP * (half + 1))
-                nc.scalar.copy(
-                    out=h_grouped_words[:, c, cols, :],
-                    in_=xt[g, c, half].rearrange("p u jj i -> p (jj i) u"),
+        def copies(u):
+            h_grouped[u] = work.tile([P, PASSES, UNIT_COLS, 4], BF16, align_bytes=64, name="h_grouped", tag="h_grouped")
+            h_grouped_words = h_grouped[u].bitcast(F32)
+            for c in range(PASSES):
+                nc.scalar.copy(out=h_grouped_words[:, c, :, :], in_=xt[u, c].rearrange("p v jj i -> p (jj i) v"))
+
+        def quantise_h(u):
+            h_codes[u] = work.tile([P, PASSES, UNIT_COLS], U32, align_bytes=64, name="h_codes", tag="h_codes", bufs=4)
+            h_scales[u] = work.tile([P, PASSES, UNIT_COLS], U8, align_bytes=64, name="h_scales", tag="h_scales", bufs=4)
+            nc.vector.quantize_mx(
+                out=h_codes[u].rearrange("p c col -> p (c col)").bitcast(FP8X4),
+                scales=h_scales[u].rearrange("p c col -> p (c col)"),
+                in_=h_grouped[u].rearrange("p c col t -> p (c col t)"),
+            )
+
+        def project(u, w, acc):
+            for c in range(PASSES):
+                nc.tensor.matmul_mx(
+                    out=acc.rearrange("p jj i -> p (jj i)"),
+                    lhsT=w_codes[:, w, c, :].bitcast(FP8X4),
+                    lhsT_scale=w_scales[:, w, c, :],
+                    rhs=h_codes[u][:, c, :].bitcast(FP8X4),
+                    rhs_scale=h_scales[u][:, c, :],
+                    start=(c == 0),
+                    stop=(c == PASSES - 1),
                 )
 
-        def quantise_h(g, c):
-            if c == 0:
-                h_codes[g] = work.tile([P, PASSES, M * GROUP], U32, align_bytes=64, name="h_codes", tag="h_codes")
-                h_scales[g] = work.tile([P, PASSES, M * GROUP], U8, align_bytes=64, name="h_scales", tag="h_scales")
-            nc.vector.quantize_mx(
-                out=h_codes[g][:, c, :].bitcast(FP8X4),
-                scales=h_scales[g][:, c, :],
-                in_=h_grouped[g][:, c].rearrange("p col t -> p (col t)"),
-            )
+        def project_z(u):
+            z_ps[u] = psum.tile([P, 2, HALF, GROUP], F32, name="z_ps", tag="z", bufs=2)
+            project(u, ZA, z_ps[u][:, 0])
+            project(u, ZB, z_ps[u][:, 1])
 
-        def project(g, w, c):
-            if c == 0:
-                acc[g, w] = psum.tile([P, M, GROUP], F32, name="acc%d" % w, tag="acc%d" % w)
-            nc.tensor.matmul_mx(
-                out=acc[g, w].rearrange("p j i -> p (j i)"),
-                lhsT=w_codes[:, w, c, :].bitcast(FP8X4),
-                lhsT_scale=w_scales[:, w, c, :],
-                rhs=h_codes[g][:, c, :].bitcast(FP8X4),
-                rhs_scale=h_scales[g][:, c, :],
-                start=(c == 0),
-                stop=(c == PASSES - 1),
-            )
+        def project_cb(u):
+            cb_ps[u] = psum.tile([P, HALF, GROUP], F32, name="cb_ps", tag="cb")
+            project(u, CB, cb_ps[u])
+
+        def project_ca(u):
+            if u % 2 == 0:
+                ca_ps[u // 2] = psum.tile([P, M, GROUP], F32, name="ca_ps", tag="ca")
+            project(u, CA, ca_ps[u // 2][:, HALF * (u % 2) : HALF * (u % 2 + 1), :])
 
         def place(g):
             return g // GROUPS_PER_BATCH, GROUP * (g % GROUPS_PER_BATCH)
 
-        def add_bias(g, s):
-            n, first = place(g)
-            for j in range(M):
-                k = M * s + j
-                nc.scalar.activation(
-                    out=z_all[n][:, k, first + s : first + s + GROUP], in_=acc[g, ZA + s][:, j, :],
-                    func=ACT.Identity, bias=bias[:, k : k + 1], scale=1.0,
-                )
+        def add_bias(u):
+            n, first = place(u // 2)
+            for s in range(2):
+                for jj in range(HALF):
+                    k = M * s + HALF * (u % 2) + jj
+                    nc.scalar.activation(
+                        out=z_all[n][:, k, first + s : first + s + GROUP], in_=z_ps[u][:, s, jj, :],
+                        func=ACT.Identity, bias=bias[:, k : k + 1], scale=1.0,
+                    )
 
-        def copy_cb(g):
-            n, first = place(g)
-            nc.scalar.copy(out=cb_all[n][:, :, first + 1 : first + 1 + GROUP], in_=acc[g, CB][:])
+        def copy_cb(u):
+            n, first = place(u // 2)
+            js = slice(HALF * (u % 2), HALF * (u % 2 + 1))
+            nc.scalar.copy(out=cb_all[n][:, js, first + 1 : first + 1 + GROUP], in_=cb_ps[u][:])
 
         def logits(g):
             n, first = place(g)
             return z_all[n][:, :, first : first + GROUP]
 
-        def max_of_8(g):
+        def maximum(g):
             max4[g] = work.tile([P, 4, GROUP], F32, name="max4", tag="max4")
             nc.vector.tensor_tensor(out=max4[g][:], in0=logits(g)[:, 0:4, :], in1=logits(g)[:, 4:8, :], op=ALU.max)
-
-        def max_of_4(g):
             max2[g] = work.tile([P, 2, GROUP], F32, name="max2", tag="max2")
             nc.vector.tensor_tensor(out=max2[g][:], in0=max4[g][:, 0:2, :], in1=max4[g][:, 2:4, :], op=ALU.max)
-
-        def max_of_2(g):
             max1[g] = work.tile([P, 1, GROUP], F32, name="max1", tag="max1")
             nc.vector.tensor_tensor(out=max1[g][:], in0=max2[g][:, 0:1, :], in1=max2[g][:, 1:2, :], op=ALU.max)
 
@@ -190,7 +206,7 @@ def tile_tokencompressor_pa_kernel(tc, H, W_a_KV, W_b_KV, W_a_Z, W_b_Z, B_a, B_b
         def times_values(g, s):
             n, first = place(g)
             ks = slice(M * s, M * (s + 1))
-            values = acc[g, CA][:] if s == 0 else cb_all[n][:, :, first : first + GROUP]
+            values = ca_ps[g][:] if s == 0 else cb_all[n][:, :, first : first + GROUP]
             nc.vector.tensor_tensor(out=terms[g][:, 1, ks, :], in0=terms[g][:, 0, ks, :], in1=values, op=ALU.mult)
 
         def sum_and_turn(g, q, total):
@@ -214,66 +230,73 @@ def tile_tokencompressor_pa_kernel(tc, H, W_a_KV, W_b_KV, W_a_Z, W_b_Z, B_a, B_b
             )
             nc.sync.dma_start(out=out_rows[:, g0:g1, :], in_=result_rows[:, g0:g1, :])
 
-        for c in range(PASSES):
-            transposes(0, c)
-            copies(0, c)
+        transposes(0)
+        copies(0)
+        transposes(1)
         regroup_w(ZA)
-        quantise_h(0, 0)
-        quantise_w(ZA)
         regroup_w(ZB)
-        quantise_h(0, 1)
+        quantise_w(ZA)
         quantise_w(ZB)
-        for s in range(2):
-            for c in range(PASSES):
-                project(0, ZA + s, c)
-            add_bias(0, s)
+        quantise_h(0)
         regroup_w(CB)
-        regroup_w(CA)
         quantise_w(CB)
+        project_z(0)
+        project_cb(0)
+        copies(1)
+        transposes(2)
+        quantise_h(1)
+        regroup_w(CA)
         quantise_w(CA)
-        transposes(1, 0)
-        for w in (CB, CA):
-            for c in range(PASSES):
-                project(0, w, c)
+        add_bias(0)
+        copy_cb(0)
+        project_z(1)
+        project_cb(1)
+        project_ca(0)
+        project_ca(1)
+        copies(2)
 
         for g in range(GROUPS):
-            ahead = g + 1 < GROUPS
-            if ahead:
-                copies(g + 1, 0)
-                transposes(g + 1, 1)
-                copies(g + 1, 1)
-            max_of_8(g)
-            max_of_4(g)
-            max_of_2(g)
-            if ahead:
-                quantise_h(g + 1, 0)
-                project(g + 1, ZA, 0)
-                project(g + 1, ZB, 0)
+            u = 2 * g + 1
+            add_bias(u)
+            copy_cb(u)
+            if u + 2 < UNITS:
+                transposes(u + 2)
+            if u + 1 < UNITS:
+                quantise_h(u + 1)
+                project_z(u + 1)
+                project_cb(u + 1)
+            if g > 0:
+                sum_and_turn(g - 1, 0, den_ps)
+            maximum(g)
             subtract_max(g, 0)
-            if ahead:
-                quantise_h(g + 1, 1)
-                project(g + 1, ZA, 1)
-                project(g + 1, ZB, 1)
+            if u + 2 < UNITS:
+                copies(u + 2)
+            if u + 3 < UNITS:
+                transposes(u + 3)
+            if u + 2 < UNITS:
+                quantise_h(u + 2)
             subtract_max(g, 1)
-            copy_cb(g)
+            if u + 1 < UNITS:
+                add_bias(u + 1)
+                copy_cb(u + 1)
+            if u + 2 < UNITS:
+                project_z(u + 2)
+                project_cb(u + 2)
+            if g > 0:
+                sum_and_turn(g - 1, 1, num_ps)
             exponentials(g, 0)
             exponentials(g, 1)
-            if ahead:
-                add_bias(g + 1, 0)
-                add_bias(g + 1, 1)
-                project(g + 1, CB, 0)
-                project(g + 1, CB, 1)
-            sum_and_turn(g, 0, den_ps)
-            if g + 2 < GROUPS:
-                transposes(g + 2, 0)
             times_values(g, 0)
-            if ahead:
-                project(g + 1, CA, 0)
-                project(g + 1, CA, 1)
+            if u + 2 < UNITS:
+                project_ca(u + 1)
+                project_ca(u + 2)
             times_values(g, 1)
-            sum_and_turn(g, 1, num_ps)
+            if u + 3 < UNITS:
+                copies(u + 3)
 
         last = GROUPS - 1
+        sum_and_turn(last, 0, den_ps)
+        sum_and_turn(last, 1, num_ps)
         reciprocal_of_sum(0, last)
         reciprocal_of_sum(last, GROUPS)
         finish(0, last)

@@ -42,7 +42,6 @@ def tile_tokencompressor_pa_kernel(tc, H, W_a_KV, W_b_KV, W_a_Z, W_b_Z, B_a, B_b
         keep = stack.enter_context(tc.tile_pool(name="keep", bufs=1))
         work = stack.enter_context(tc.tile_pool(name="work", bufs=2))
         psum = stack.enter_context(tc.psum_pool(name="psum", bufs=1))
-        stack.enter_context(tc.manual_schedule())
 
         h_raw = [keep.tile([P, M, D], BF16, name="h_raw%d" % g) for g in range(GROUPS)]
         w_raw = keep.tile([P, 4, PASSES, 4, CH], BF16)

@@ -42,6 +42,7 @@ def tile_tokencompressor_pa_kernel(tc, H, W_a_KV, W_b_KV, W_a_Z, W_b_Z, B_a, B_b
         keep = stack.enter_context(tc.tile_pool(name="keep", bufs=1))
         work = stack.enter_context(tc.tile_pool(name="work", bufs=2))
         psum = stack.enter_context(tc.psum_pool(name="psum", bufs=1))
+        stack.enter_context(tc.manual_schedule())
 
         h_raw = [keep.tile([P, M, D], BF16, name="h_raw%d" % g) for g in range(GROUPS)]
         w_raw = keep.tile([P, 4, PASSES, 4, CH], BF16)
@@ -260,18 +261,20 @@ def tile_tokencompressor_pa_kernel(tc, H, W_a_KV, W_b_KV, W_a_Z, W_b_Z, B_a, B_b
             copy_cb(u)
             if u + 2 < UNITS:
                 transposes(u + 2)
+            if g > 0:
+                sum_and_turn(g - 1, 0, den_ps)
             if u + 1 < UNITS:
                 quantise_h(u + 1)
                 project_z(u + 1)
                 project_cb(u + 1)
-            if g > 0:
-                sum_and_turn(g - 1, 0, den_ps)
             maximum(g)
             subtract_max(g, 0)
             if u + 2 < UNITS:
                 copies(u + 2)
             if u + 3 < UNITS:
                 transposes(u + 3)
+            if g > 0:
+                sum_and_turn(g - 1, 1, num_ps)
             if u + 2 < UNITS:
                 quantise_h(u + 2)
             subtract_max(g, 1)
@@ -281,8 +284,6 @@ def tile_tokencompressor_pa_kernel(tc, H, W_a_KV, W_b_KV, W_a_Z, W_b_Z, B_a, B_b
             if u + 2 < UNITS:
                 project_z(u + 2)
                 project_cb(u + 2)
-            if g > 0:
-                sum_and_turn(g - 1, 1, num_ps)
             exponentials(g, 0)
             exponentials(g, 1)
             times_values(g, 0)

from contextlib import ExitStack

import concourse.mybir as mybir
from concourse.masks import make_identity

F32 = mybir.dt.float32
BF16 = mybir.dt.bfloat16
U32 = mybir.dt.uint32
U8 = mybir.dt.uint8
FP8X4 = mybir.dt.float8_e4m3fn_x4
ACT = mybir.ActivationFunctionType
ALU = mybir.AluOpType

P = 128
BATCH = 2
TOKENS = 1024
D = 1024
CH = 128
M = 4
K_PASS = 512
PASSES = D // K_PASS
GROUP = 128
GROUPS = BATCH * TOKENS // (M * GROUP)
GROUPS_PER_BATCH = GROUPS // BATCH
BLOCKS = TOKENS // M
HALF = M // 2
UNITS = 2 * GROUPS
UNIT_COLS = HALF * GROUP
NEG = -1e30
ZA, ZB, CA, CB = 0, 1, 2, 3

FLOPS = 2 * BATCH * TOKENS * D * 4 * CH


def tile_tokencompressor_pa_kernel(tc, H, W_a_KV, W_b_KV, W_a_Z, W_b_Z, B_a, B_b, out):
    nc = tc.nc
    weights = [W_a_Z, W_b_Z, W_a_KV, W_b_KV]
    h_groups = H.flatten_outer_dims().rearrange("(g i j) d -> g i j d", i=GROUP, j=M)
    out_rows = out.flatten_outer_dims().rearrange("(g i) c -> i g c", i=GROUP)

    with ExitStack() as stack:
        keep = stack.enter_context(tc.tile_pool(name="keep", bufs=1))
        work = stack.enter_context(tc.tile_pool(name="work", bufs=2))
        psum = stack.enter_context(tc.psum_pool(name="psum", bufs=1))
        stack.enter_context(tc.manual_schedule())

        h_raw = [keep.tile([P, M, D], BF16, name="h_raw%d" % g) for g in range(GROUPS)]
        w_raw = keep.tile([P, 4, PASSES, 4, CH], BF16)
        bias_rows = keep.tile([P, P], BF16)

        def load_h(u):
            js = slice(HALF * (u % 2), HALF * (u % 2 + 1))
            nc.sync.dma_start(out=h_raw[u // 2][:, js, :], in_=h_groups[u // 2][:, js, :])

        def load_w(w):
            nc.sync.dma_start(
                out=w_raw[:, w].rearrange("p c (u e) n -> p c u e n", e=2),
                in_=weights[w].rearrange("(c u p e) n -> p c u e n", c=PASSES, u=2, e=2),
            )

        nc.vector.memset(bias_rows[:], 0.0)
        nc.sync.dma_start(out=bias_rows[0:M, :], in_=B_a)
        nc.sync.dma_start(out=bias_rows[M : 2 * M, :], in_=B_b)
        load_h(0)
        load_w(ZA)
        load_w(ZB)
        load_h(1)
        load_w(CB)
        load_w(CA)
        for u in range(2, UNITS):
            load_h(u)

        ident = keep.tile([P, P], F32)
        make_identity(nc, ident[:])

        z_all = [keep.tile([P, 2 * M, BLOCKS + 1], F32, name="z_all%d" % n) for n in range(BATCH)]
        cb_all = [keep.tile([P, M, BLOCKS + 1], F32, name="cb_all%d" % n) for n in range(BATCH)]
        for n in range(BATCH):
            nc.vector.memset(z_all[n][:, M : 2 * M, 0:1], NEG)
            nc.vector.memset(cb_all[n][:, :, 0:1], 0.0)
        den_ps = psum.tile([P, GROUPS, CH], F32)
        num_ps = psum.tile([P, GROUPS, CH], F32)

        bias_rows32 = keep.tile([P, P], F32)
        nc.vector.tensor_copy(out=bias_rows32[:], in_=bias_rows[:])
        bias_ps = psum.tile([P, P], F32, tag="ca")
        nc.tensor.transpose(out=bias_ps[:], in_=bias_rows32[:], identity=ident[:])
        bias = keep.tile([P, 2 * M], F32)
        nc.vector.tensor_copy(out=bias[:], in_=bias_ps[:, 0 : 2 * M])

        w_grouped = keep.tile([P, 4, PASSES, CH, 4], BF16, align_bytes=64)
        w_codes = keep.tile([P, 4, PASSES, CH], U32, align_bytes=64)
        w_scales = keep.tile([P, 4, PASSES, CH], U8, align_bytes=64)

        def regroup_w(w):
            nc.vector.tensor_copy(out=w_grouped[:, w], in_=w_raw[:, w].rearrange("p c t n -> p c n t"))

        def quantise_w(w):
            nc.vector.quantize_mx(
                out=w_codes[:, w].rearrange("p c n -> p (c n)").bitcast(FP8X4),
                scales=w_scales[:, w].rearrange("p c n -> p (c n)"),
                in_=w_grouped[:, w].rearrange("p c n t -> p (c n t)"),
            )

        xt, h_grouped, h_codes, h_scales = {}, {}, {}, {}
        z_ps, cb_ps, ca_ps = {}, {}, {}
        max4, max2, max1, terms = {}, {}, {}, {}

        def transposes(u):
            h_words = h_raw[u // 2].bitcast(F32)
            for c in range(PASSES):
                xt[u, c] = psum.tile([P, 2, HALF, GROUP], F32, name="xt", tag="xt", bufs=2)
                for v in range(2):
                    for jj in range(HALF):
                        first = 256 * c + 128 * v
                        nc.tensor.transpose(
                            out=xt[u, c][:, v, jj, :],
                            in_=h_words[:, HALF * (u % 2) + jj, first : first + 128],
                            identity=ident[:],
                        )

        def copies(u):
            h_grouped[u] = work.tile([P, PASSES, UNIT_COLS, 4], BF16, align_bytes=64, name="h_grouped", tag="h_grouped")
            h_grouped_words = h_grouped[u].bitcast(F32)
            for c in range(PASSES):
                nc.scalar.copy(out=h_grouped_words[:, c, :, :], in_=xt[u, c].rearrange("p v jj i -> p (jj i) v"))

        def quantise_h(u):
            h_codes[u] = work.tile([P, PASSES, UNIT_COLS], U32, align_bytes=64, name="h_codes", tag="h_codes", bufs=4)
            h_scales[u] = work.tile([P, PASSES, UNIT_COLS], U8, align_bytes=64, name="h_scales", tag="h_scales", bufs=4)
            nc.vector.quantize_mx(
                out=h_codes[u].rearrange("p c col -> p (c col)").bitcast(FP8X4),
                scales=h_scales[u].rearrange("p c col -> p (c col)"),
                in_=h_grouped[u].rearrange("p c col t -> p (c col t)"),
            )

        def project(u, w, acc):
            for c in range(PASSES):
                nc.tensor.matmul_mx(
                    out=acc.rearrange("p jj i -> p (jj i)"),
                    lhsT=w_codes[:, w, c, :].bitcast(FP8X4),
                    lhsT_scale=w_scales[:, w, c, :],
                    rhs=h_codes[u][:, c, :].bitcast(FP8X4),
                    rhs_scale=h_scales[u][:, c, :],
                    start=(c == 0),
                    stop=(c == PASSES - 1),
                )

        def project_z(u):
            z_ps[u] = psum.tile([P, 2, HALF, GROUP], F32, name="z_ps", tag="z", bufs=2)
            project(u, ZA, z_ps[u][:, 0])
            project(u, ZB, z_ps[u][:, 1])

        def project_cb(u):
            cb_ps[u] = psum.tile([P, HALF, GROUP], F32, name="cb_ps", tag="cb")
            project(u, CB, cb_ps[u])

        def project_ca(u):
            if u % 2 == 0:
                ca_ps[u // 2] = psum.tile([P, M, GROUP], F32, name="ca_ps", tag="ca")
            project(u, CA, ca_ps[u // 2][:, HALF * (u % 2) : HALF * (u % 2 + 1), :])

        def place(g):
            return g // GROUPS_PER_BATCH, GROUP * (g % GROUPS_PER_BATCH)

        def add_bias(u):
            n, first = place(u // 2)
            for s in range(2):
                for jj in range(HALF):
                    k = M * s + HALF * (u % 2) + jj
                    nc.scalar.activation(
                        out=z_all[n][:, k, first + s : first + s + GROUP], in_=z_ps[u][:, s, jj, :],
                        func=ACT.Identity, bias=bias[:, k : k + 1], scale=1.0,
                    )

        def copy_cb(u):
            n, first = place(u // 2)
            js = slice(HALF * (u % 2), HALF * (u % 2 + 1))
            nc.scalar.copy(out=cb_all[n][:, js, first + 1 : first + 1 + GROUP], in_=cb_ps[u][:])

        def logits(g):
            n, first = place(g)
            return z_all[n][:, :, first : first + GROUP]

        def maximum(g):
            max4[g] = work.tile([P, 4, GROUP], F32, name="max4", tag="max4")
            nc.vector.tensor_tensor(out=max4[g][:], in0=logits(g)[:, 0:4, :], in1=logits(g)[:, 4:8, :], op=ALU.max)
            max2[g] = work.tile([P, 2, GROUP], F32, name="max2", tag="max2")
            nc.vector.tensor_tensor(out=max2[g][:], in0=max4[g][:, 0:2, :], in1=max4[g][:, 2:4, :], op=ALU.max)
            max1[g] = work.tile([P, 1, GROUP], F32, name="max1", tag="max1")
            nc.vector.tensor_tensor(out=max1[g][:], in0=max2[g][:, 0:1, :], in1=max2[g][:, 1:2, :], op=ALU.max)

        def subtract_max(g, s):
            if s == 0:
                terms[g] = work.tile([P, 2, 2 * M, GROUP], F32, name="terms", tag="terms")
            ks = slice(M * s, M * (s + 1))
            nc.vector.tensor_tensor(
                out=terms[g][:, 0, ks, :], in0=logits(g)[:, ks, :],
                in1=max1[g].to_broadcast([P, M, GROUP]), op=ALU.subtract,
            )

        def exponentials(g, s):
            ks = slice(M * s, M * (s + 1))
            nc.scalar.activation(out=terms[g][:, 0, ks, :], in_=terms[g][:, 0, ks, :], func=ACT.Exp)

        def times_values(g, s):
            n, first = place(g)
            ks = slice(M * s, M * (s + 1))
            values = ca_ps[g][:] if s == 0 else cb_all[n][:, :, first : first + GROUP]
            nc.vector.tensor_tensor(out=terms[g][:, 1, ks, :], in0=terms[g][:, 0, ks, :], in1=values, op=ALU.mult)

        def sum_and_turn(g, q, total):
            for k in range(2 * M):
                nc.tensor.matmul(
                    out=total[:, g, :], lhsT=terms[g][:, q, k, :], rhs=ident[:], is_transpose=True,
                    start=(k == 0), stop=(k == 2 * M - 1),
                )

        rsqrt = keep.tile([P, GROUPS, CH], F32)
        recip = keep.tile([P, GROUPS, CH], F32)
        result_rows = keep.tile([P, GROUPS, CH], F32)

        def reciprocal_of_sum(g0, g1):
            nc.scalar.activation(out=rsqrt[:, g0:g1, :], in_=den_ps[:, g0:g1, :], func=ACT.Abs_reciprocal_sqrt)
            nc.scalar.activation(out=recip[:, g0:g1, :], in_=rsqrt[:, g0:g1, :], func=ACT.Square)

        def finish(g0, g1):
            nc.vector.tensor_tensor(
                out=result_rows[:, g0:g1, :], in0=num_ps[:, g0:g1, :], in1=recip[:, g0:g1, :], op=ALU.mult
            )
            nc.sync.dma_start(out=out_rows[:, g0:g1, :], in_=result_rows[:, g0:g1, :])

        transposes(0)
        copies(0)
        transposes(1)
        regroup_w(ZA)
        regroup_w(ZB)
        quantise_w(ZA)
        quantise_w(ZB)
        quantise_h(0)
        regroup_w(CB)
        quantise_w(CB)
        project_z(0)
        project_cb(0)
        copies(1)
        transposes(2)
        quantise_h(1)
        regroup_w(CA)
        quantise_w(CA)
        add_bias(0)
        copy_cb(0)
        project_z(1)
        project_cb(1)
        project_ca(0)
        project_ca(1)
        copies(2)

        for g in range(GROUPS):
            u = 2 * g + 1
            add_bias(u)
            copy_cb(u)
            if u + 2 < UNITS:
                transposes(u + 2)
            if g > 0:
                sum_and_turn(g - 1, 0, den_ps)
            if u + 1 < UNITS:
                quantise_h(u + 1)
                project_z(u + 1)
                project_cb(u + 1)
            maximum(g)
            subtract_max(g, 0)
            if u + 2 < UNITS:
                copies(u + 2)
            if u + 3 < UNITS:
                transposes(u + 3)
            if g > 0:
                sum_and_turn(g - 1, 1, num_ps)
            if u + 2 < UNITS:
                quantise_h(u + 2)
            subtract_max(g, 1)
            if u + 1 < UNITS:
                add_bias(u + 1)
                copy_cb(u + 1)
            if u + 2 < UNITS:
                project_z(u + 2)
                project_cb(u + 2)
            exponentials(g, 0)
            exponentials(g, 1)
            times_values(g, 0)
            if u + 2 < UNITS:
                project_ca(u + 1)
                project_ca(u + 2)
            times_values(g, 1)
            if u + 3 < UNITS:
                copies(u + 3)

        last = GROUPS - 1
        sum_and_turn(last, 0, den_ps)
        sum_and_turn(last, 1, num_ps)
        reciprocal_of_sum(0, last)
        reciprocal_of_sum(last, GROUPS)
        finish(0, last)
        finish(last, GROUPS)
